import numpy as np
import ml_dtypes


def mxq(x, axis, fmt="e4m3"):
    dtype, down = {"e4m3": (ml_dtypes.float8_e4m3fn, 7), "e5m2": (ml_dtypes.float8_e5m2, 14)}[fmt]
    v = np.moveaxis(np.asarray(x, np.float32).astype(ml_dtypes.bfloat16).astype(np.float64), axis, -1)
    blocks = v.reshape(v.shape[:-1] + (-1, 32))
    amax = np.abs(blocks).max(-1, keepdims=True)
    byte = np.maximum(np.where(amax > 0, np.frexp(amax)[1] - 1 + 127, 0) - down, 1)
    scale = np.exp2(byte - 127.0)
    codes = (blocks / scale).astype(np.float32).astype(dtype).astype(np.float64)
    return np.moveaxis((codes * scale).reshape(v.shape), -1, axis)


WIDE = False


def mx_kscale(k):
    if not WIDE:
        return np.ones(k)
    levels = np.array([20, -20, 10, -10, 0])
    a = np.random.permutation(np.resize(levels, k // 512 * 4)).reshape(k // 512, 4)
    idx = np.arange(k)
    return np.exp2(a[idx // 512, idx % 128 // 32])


BF16 = ml_dtypes.bfloat16


def bf(x):
    return np.asarray(x, np.float32).astype(BF16)


def f64(x):
    return np.asarray(x).astype(np.float64)


N1, N2, N3, R1, R = 32, 32, 512, 512, 8192


def setup_inputs():
    s = mx_kscale(N1 * N2)[::N2]
    g = R ** (-1.0 / 6.0)
    X = np.random.standard_normal((N1, N2, N3))
    A = np.random.standard_normal((N1, R)) * g * s[:, None]
    B = np.random.standard_normal((N2, R)) * g
    C = np.random.standard_normal((N3, R)) * g
    go = np.random.standard_normal((N1, N2, N3)) * np.exp2(np.random.randint(-12, 1, (N1, N2, 1))) * 4.0 / s[:, None, None]
    return {"X": bf(X), "A": bf(A), "B": bf(B), "C": bf(C), "grad_out": bf(go)}


def reference(X, A, B, C, grad_out):
    p = (f64(A)[:, None, :] * f64(B)[None, :, :]).reshape(N1 * N2, R)
    g = f64(grad_out).reshape(N1 * N2, N3)
    return mxq(g, 0, "e5m2").T @ mxq(p, 0, "e4m3")

@@ -1,0 +1,165 @@
+from contextlib import ExitStack
+
+import concourse.mybir as mybir
+from concourse.masks import make_identity
+
+BF16 = mybir.dt.bfloat16
+F32 = mybir.dt.float32
+U32 = mybir.dt.uint32
+U8 = mybir.dt.uint8
+E4M3_X4 = mybir.dt.float8_e4m3fn_x4
+E5M2_X4 = mybir.dt.float8_e5m2_x4
+
+N1, N2, N3, R = 32, 32, 512, 8192
+P = 128
+PACK = 4
+K_PASS = P * PACK
+PASSES = (N1 * N2) // K_PASS
+I_PER_PASS = K_PASS // N2
+Q = N2 // PACK
+M_TILES = N3 // P
+CHUNK = 512
+N_CHUNKS = R // CHUNK
+A_SPLIT = P // N1
+A_COLS = R // A_SPLIT
+
+FLOPS = 2 * N1 * N2 * N3 * R
+BYTES = 2 * (N1 * R + N2 * R + N1 * N2 * N3) + 4 * N3 * R
+
+
+def regroup(copy, grouped, planar):
+    copy(
+        out=grouped.rearrange("p (n i) t -> p n t i", i=4),
+        in_=planar.rearrange("p t (n i) -> p n t i", i=4),
+    )
+
+
+def tile_recon_loss_pa_kernel(tc, X, A, B, C, grad_out, out):
+    nc = tc.nc
+    with ExitStack() as ctx:
+        ctx.enter_context(tc.manual_schedule())
+        keep = ctx.enter_context(tc.tile_pool(name="keep", bufs=1))
+        work = ctx.enter_context(tc.tile_pool(name="work", bufs=3))
+        stage = ctx.enter_context(tc.tile_pool(name="stage", bufs=12))
+        a_psum = ctx.enter_context(tc.psum_pool(name="a_psum", bufs=2))
+        acc_psum = ctx.enter_context(tc.psum_pool(name="acc_psum", bufs=6))
+
+        a_rows = keep.tile([P, A_COLS], BF16)
+        a_by_quarter = A.rearrange("i (h r) -> (i h) r", h=A_SPLIT)
+        b_planes = keep.tile([P, PACK, R], BF16)
+        b_by_plane = B.rearrange("(q t) r -> t q r", t=PACK)
+        g_rows = keep.tile([P, PASSES, PACK, N3], BF16)
+        g_by_pass = grad_out.rearrange("i j k -> (i j) k").rearrange(
+            "(c p t) k -> c p t k", c=PASSES, t=PACK
+        )
+
+        def load_a(n):
+            cols = slice(n * CHUNK, (n + 1) * CHUNK)
+            nc.sync.dma_start(out=a_rows[:, cols], in_=a_by_quarter[:, cols])
+
+        def load_b(n):
+            cols = slice(n * CHUNK, (n + 1) * CHUNK)
+            for t in range(PACK):
+                nc.sync.dma_start(
+                    out=b_planes[:, t, cols],
+                    in_=b_by_plane[t, :, cols].unsqueeze(0).to_broadcast([P // Q, Q, CHUNK]),
+                )
+
+        load_a(0)
+        load_b(0)
+        load_a(1)
+        load_b(1)
+        for c in range(PASSES):
+            nc.sync.dma_start(out=g_rows[:, c], in_=g_by_pass[c])
+        for n in range(2, N_CHUNKS):
+            if n * CHUNK < A_COLS:
+                load_a(n)
+            load_b(n)
+
+        ident = keep.tile([P, P], BF16)
+        make_identity(nc, ident[:])
+        spread = keep.tile([P, A_SPLIT, PASSES, P], BF16)
+        nc.vector.tensor_copy(
+            out=spread[:].rearrange("k h c (g e) -> k h (c g) e", e=Q),
+            in_=ident[:]
+            .rearrange("k (m h) -> k h m", h=A_SPLIT)
+            .unsqueeze(3)
+            .to_broadcast([P, A_SPLIT, N1, Q]),
+        )
+
+        g_grouped = keep.tile([P, PASSES, N3, PACK], BF16, align_bytes=64)
+        g_codes = keep.tile([P, PASSES, N3], U32, align_bytes=64)
+        g_scales = keep.tile([P, PASSES, N3], U8, align_bytes=64)
+
+        def prepare_g():
+            regroup(nc.vector.tensor_copy, g_grouped[:, 0], g_rows[:, 0])
+            regroup(nc.scalar.copy, g_grouped[:, 1], g_rows[:, 1])
+
+        def quantise_g():
+            nc.vector.quantize_mx(
+                out=g_codes[:].rearrange("p c k -> p (c k)").bitcast(E5M2_X4),
+                scales=g_scales[:].rearrange("p c k -> p (c k)"),
+                in_=g_grouped[:].rearrange("p c k t -> p (c k t)"),
+            )
+
+        def products(n):
+            h, a_col = divmod(n * CHUNK, A_COLS)
+            a_spread = a_psum.tile([P, PASSES, CHUNK], BF16)
+            for c in range(PASSES):
+                nc.tensor.matmul(
+                    out=a_spread[:, c, :],
+                    lhsT=spread[:, h, c, :],
+                    rhs=a_rows[:, a_col : a_col + CHUNK],
+                    start=True,
+                    stop=True,
+                )
+            shape = [P, PASSES, PACK, CHUNK]
+            planar = work.tile(shape, BF16)
+            nc.vector.tensor_tensor(
+                out=planar[:],
+                in0=b_planes[:, :, n * CHUNK : (n + 1) * CHUNK].unsqueeze(1).to_broadcast(shape),
+                in1=a_spread[:].unsqueeze(2).to_broadcast(shape),
+                op=mybir.AluOpType.mult,
+            )
+            grouped = work.tile([P, PASSES, CHUNK, PACK], BF16, align_bytes=64)
+            regroup(nc.vector.tensor_copy, grouped[:, 0], planar[:, 0])
+            regroup(nc.scalar.copy, grouped[:, 1], planar[:, 1])
+            return grouped
+
+        def multiply(n, grouped):
+            codes = work.tile([P, PASSES, CHUNK], U32, align_bytes=64)
+            scales = work.tile([P, PASSES, CHUNK], U8, align_bytes=64)
+            nc.vector.quantize_mx(
+                out=codes[:].rearrange("p c r -> p (c r)").bitcast(E4M3_X4),
+                scales=scales[:].rearrange("p c r -> p (c r)"),
+                in_=grouped[:].rearrange("p c r t -> p (c r t)"),
+            )
+            for m in range(M_TILES):
+                rows = slice(m * P, (m + 1) * P)
+                acc = acc_psum.tile([P, CHUNK], F32)
+                for c in range(PASSES):
+                    nc.tensor.matmul_mx(
+                        out=acc[:],
+                        lhsT=g_codes[:, c, rows].bitcast(E5M2_X4),
+                        lhsT_scale=g_scales[:, c, rows],
+                        rhs=codes[:, c, :].bitcast(E4M3_X4),
+                        rhs_scale=scales[:, c, :],
+                        start=(c == 0),
+                        stop=(c == PASSES - 1),
+                    )
+                result = stage.tile([P, CHUNK], F32)
+                if n == N_CHUNKS - 1 and m % 2 == 1:
+                    nc.vector.tensor_copy(out=result[:], in_=acc[:])
+                else:
+                    nc.scalar.copy(out=result[:], in_=acc[:])
+                nc.sync.dma_start(out=out[rows, n * CHUNK : (n + 1) * CHUNK], in_=result[:])
+
+        waiting = products(0)
+        prepare_g()
+        for n in range(1, N_CHUNKS):
+            following = products(n)
+            if n == 1:
+                quantise_g()
+            multiply(n - 1, waiting)
+            waiting = following
+        multiply(N_CHUNKS - 1, waiting)

@@ -27,11 +27,21 @@ FLOPS = 2 * N1 * N2 * N3 * R
 BYTES = 2 * (N1 * R + N2 * R + N1 * N2 * N3) + 4 * N3 * R
 
 
-def regroup(copy, grouped, planar):
-    copy(
-        out=grouped.rearrange("p (n i) t -> p n t i", i=4),
-        in_=planar.rearrange("p t (n i) -> p n t i", i=4),
+def regroup_views(grouped, planar):
+    return (
+        grouped.rearrange("p (n i) t -> p n t i", i=4),
+        planar.rearrange("p t (n i) -> p n t i", i=4),
     )
+
+
+def regroup_on_vector(nc, grouped, planar):
+    dst, src = regroup_views(grouped, planar)
+    nc.vector.tensor_copy(out=dst, in_=src)
+
+
+def regroup_on_scalar(nc, grouped, planar):
+    dst, src = regroup_views(grouped, planar)
+    nc.scalar.copy(out=dst, in_=src)
 
 
 def tile_recon_loss_pa_kernel(tc, X, A, B, C, grad_out, out):
@@ -67,11 +77,9 @@ def tile_recon_loss_pa_kernel(tc, X, A, B, C, grad_out, out):
 
         load_a(0)
         load_b(0)
-        load_a(1)
-        load_b(1)
         for c in range(PASSES):
             nc.sync.dma_start(out=g_rows[:, c], in_=g_by_pass[c])
-        for n in range(2, N_CHUNKS):
+        for n in range(1, N_CHUNKS):
             if n * CHUNK < A_COLS:
                 load_a(n)
             load_b(n)
@@ -92,8 +100,8 @@ def tile_recon_loss_pa_kernel(tc, X, A, B, C, grad_out, out):
         g_scales = keep.tile([P, PASSES, N3], U8, align_bytes=64)
 
         def prepare_g():
-            regroup(nc.vector.tensor_copy, g_grouped[:, 0], g_rows[:, 0])
-            regroup(nc.scalar.copy, g_grouped[:, 1], g_rows[:, 1])
+            regroup_on_vector(nc, g_grouped[:, 0], g_rows[:, 0])
+            regroup_on_scalar(nc, g_grouped[:, 1], g_rows[:, 1])
 
         def quantise_g():
             nc.vector.quantize_mx(
@@ -102,7 +110,7 @@ def tile_recon_loss_pa_kernel(tc, X, A, B, C, grad_out, out):
                 in_=g_grouped[:].rearrange("p c k t -> p (c k t)"),
             )
 
-        def products(n):
+        def spread_a(n):
             h, a_col = divmod(n * CHUNK, A_COLS)
             a_spread = a_psum.tile([P, PASSES, CHUNK], BF16)
             for c in range(PASSES):
@@ -113,6 +121,9 @@ def tile_recon_loss_pa_kernel(tc, X, A, B, C, grad_out, out):
                     start=True,
                     stop=True,
                 )
+            return a_spread
+
+        def products(n, a_spread):
             shape = [P, PASSES, PACK, CHUNK]
             planar = work.tile(shape, BF16)
             nc.vector.tensor_tensor(
@@ -121,12 +132,9 @@ def tile_recon_loss_pa_kernel(tc, X, A, B, C, grad_out, out):
                 in1=a_spread[:].unsqueeze(2).to_broadcast(shape),
                 op=mybir.AluOpType.mult,
             )
-            grouped = work.tile([P, PASSES, CHUNK, PACK], BF16, align_bytes=64)
-            regroup(nc.vector.tensor_copy, grouped[:, 0], planar[:, 0])
-            regroup(nc.scalar.copy, grouped[:, 1], planar[:, 1])
-            return grouped
+            return planar
 
-        def multiply(n, grouped):
+        def quantise(grouped):
             codes = work.tile([P, PASSES, CHUNK], U32, align_bytes=64)
             scales = work.tile([P, PASSES, CHUNK], U8, align_bytes=64)
             nc.vector.quantize_mx(
@@ -134,6 +142,9 @@ def tile_recon_loss_pa_kernel(tc, X, A, B, C, grad_out, out):
                 scales=scales[:].rearrange("p c r -> p (c r)"),
                 in_=grouped[:].rearrange("p c r t -> p (c r t)"),
             )
+            return codes, scales
+
+        def multiply(n, codes, scales):
             for m in range(M_TILES):
                 rows = slice(m * P, (m + 1) * P)
                 acc = acc_psum.tile([P, CHUNK], F32)
@@ -154,12 +165,22 @@ def tile_recon_loss_pa_kernel(tc, X, A, B, C, grad_out, out):
                     nc.scalar.copy(out=result[:], in_=acc[:])
                 nc.sync.dma_start(out=out[rows, n * CHUNK : (n + 1) * CHUNK], in_=result[:])
 
-        waiting = products(0)
-        prepare_g()
-        for n in range(1, N_CHUNKS):
-            following = products(n)
+        a_spread = {0: spread_a(0)}
+        grouped = {}
+        for n in range(N_CHUNKS + 1):
+            if n + 1 < N_CHUNKS:
+                a_spread[n + 1] = spread_a(n + 1)
+            if n < N_CHUNKS:
+                planar = products(n, a_spread[n])
+                grouped[n] = work.tile([P, PASSES, CHUNK, PACK], BF16, align_bytes=64, name="grouped")
+                regroup_on_scalar(nc, grouped[n][:, 1], planar[:, 1])
+            if n == 0:
+                prepare_g()
             if n == 1:
                 quantise_g()
-            multiply(n - 1, waiting)
-            waiting = following
-        multiply(N_CHUNKS - 1, waiting)
+            if n >= 1:
+                codes, scales = quantise(grouped[n - 1])
+            if n < N_CHUNKS:
+                regroup_on_vector(nc, grouped[n][:, 0], planar[:, 0])
+            if n >= 1:
+                multiply(n - 1, codes, scales)

@@ -39,6 +39,17 @@ def regroup_on_vector(nc, grouped, planar):
     nc.vector.tensor_copy(out=dst, in_=src)
 
 
+def regroup_on_gpsimd(nc, grouped, planar):
+    nc.gpsimd.tensor_scalar(
+        out=grouped,
+        in0=planar.rearrange("p t w -> p w t"),
+        scalar1=1.0,
+        scalar2=0.0,
+        op0=mybir.AluOpType.mult,
+        op1=mybir.AluOpType.add,
+    )
+
+
 def regroup_on_scalar(nc, grouped, planar):
     dst, src = regroup_views(grouped, planar)
     nc.scalar.copy(out=dst, in_=src)
@@ -49,7 +60,7 @@ def tile_recon_loss_pa_kernel(tc, X, A, B, C, grad_out, out):
     with ExitStack() as ctx:
         ctx.enter_context(tc.manual_schedule())
         keep = ctx.enter_context(tc.tile_pool(name="keep", bufs=1))
-        work = ctx.enter_context(tc.tile_pool(name="work", bufs=3))
+        work = ctx.enter_context(tc.tile_pool(name="work", bufs=4))
         stage = ctx.enter_context(tc.tile_pool(name="stage", bufs=12))
         a_psum = ctx.enter_context(tc.psum_pool(name="a_psum", bufs=2))
         acc_psum = ctx.enter_context(tc.psum_pool(name="acc_psum", bufs=6))
@@ -144,7 +155,8 @@ def tile_recon_loss_pa_kernel(tc, X, A, B, C, grad_out, out):
             )
             return codes, scales
 
-        def multiply(n, codes, scales):
+        def multiply(codes, scales):
+            banks = []
             for m in range(M_TILES):
                 rows = slice(m * P, (m + 1) * P)
                 acc = acc_psum.tile([P, CHUNK], F32)
@@ -158,29 +170,36 @@ def tile_recon_loss_pa_kernel(tc, X, A, B, C, grad_out, out):
                         start=(c == 0),
                         stop=(c == PASSES - 1),
                     )
-                result = stage.tile([P, CHUNK], F32)
-                if n == N_CHUNKS - 1 and m % 2 == 1:
-                    nc.vector.tensor_copy(out=result[:], in_=acc[:])
-                else:
-                    nc.scalar.copy(out=result[:], in_=acc[:])
-                nc.sync.dma_start(out=out[rows, n * CHUNK : (n + 1) * CHUNK], in_=result[:])
+                banks.append(acc)
+            return banks
+
+        def store(n, m, copy, acc):
+            result = stage.tile([P, CHUNK], F32)
+            copy(out=result[:], in_=acc[:])
+            nc.sync.dma_start(
+                out=out[m * P : (m + 1) * P, n * CHUNK : (n + 1) * CHUNK], in_=result[:]
+            )
 
         a_spread = {0: spread_a(0)}
         grouped = {}
-        for n in range(N_CHUNKS + 1):
+        banks = {}
+        for n in range(N_CHUNKS + 3):
             if n + 1 < N_CHUNKS:
                 a_spread[n + 1] = spread_a(n + 1)
             if n < N_CHUNKS:
                 planar = products(n, a_spread[n])
                 grouped[n] = work.tile([P, PASSES, CHUNK, PACK], BF16, align_bytes=64, name="grouped")
+                regroup_on_gpsimd(nc, grouped[n][:, 0], planar[:, 0])
                 regroup_on_scalar(nc, grouped[n][:, 1], planar[:, 1])
             if n == 0:
                 prepare_g()
-            if n == 1:
+            if n == 2:
                 quantise_g()
-            if n >= 1:
-                codes, scales = quantise(grouped[n - 1])
-            if n < N_CHUNKS:
-                regroup_on_vector(nc, grouped[n][:, 0], planar[:, 0])
-            if n >= 1:
-                multiply(n - 1, codes, scales)
+            if 0 <= n - 2 < N_CHUNKS:
+                codes, scales = quantise(grouped[n - 2])
+            if 0 <= n - 3 < N_CHUNKS:
+                store(n - 3, M_TILES - 1, nc.vector.tensor_copy, banks[n - 3][M_TILES - 1])
+            if 0 <= n - 2 < N_CHUNKS:
+                banks[n - 2] = multiply(codes, scales)
+                for m in range(M_TILES - 1):
+                    store(n - 2, m, nc.scalar.copy, banks[n - 2][m])

@@ -15,13 +15,14 @@ P = 128
 PACK = 4
 K_PASS = P * PACK
 PASSES = (N1 * N2) // K_PASS
-I_PER_PASS = K_PASS // N2
 Q = N2 // PACK
 M_TILES = N3 // P
 CHUNK = 512
 N_CHUNKS = R // CHUNK
 A_SPLIT = P // N1
 A_COLS = R // A_SPLIT
+HALF = CHUNK // 2
+B_AHEAD = 6
 
 FLOPS = 2 * N1 * N2 * N3 * R
 BYTES = 2 * (N1 * R + N2 * R + N1 * N2 * N3) + 4 * N3 * R
@@ -39,17 +40,6 @@ def regroup_on_vector(nc, grouped, planar):
     nc.vector.tensor_copy(out=dst, in_=src)
 
 
-def regroup_on_gpsimd(nc, grouped, planar):
-    nc.gpsimd.tensor_scalar(
-        out=grouped,
-        in0=planar.rearrange("p t w -> p w t"),
-        scalar1=1.0,
-        scalar2=0.0,
-        op0=mybir.AluOpType.mult,
-        op1=mybir.AluOpType.add,
-    )
-
-
 def regroup_on_scalar(nc, grouped, planar):
     dst, src = regroup_views(grouped, planar)
     nc.scalar.copy(out=dst, in_=src)
@@ -60,40 +50,30 @@ def tile_recon_loss_pa_kernel(tc, X, A, B, C, grad_out, out):
     with ExitStack() as ctx:
         ctx.enter_context(tc.manual_schedule())
         keep = ctx.enter_context(tc.tile_pool(name="keep", bufs=1))
-        work = ctx.enter_context(tc.tile_pool(name="work", bufs=4))
+        work = ctx.enter_context(tc.tile_pool(name="work", bufs=3))
         stage = ctx.enter_context(tc.tile_pool(name="stage", bufs=12))
-        a_psum = ctx.enter_context(tc.psum_pool(name="a_psum", bufs=2))
-        acc_psum = ctx.enter_context(tc.psum_pool(name="acc_psum", bufs=6))
+        a0_psum = ctx.enter_context(tc.psum_pool(name="a0_psum", bufs=2))
+        a1_psum = ctx.enter_context(tc.psum_pool(name="a1_psum", bufs=1))
+        acc_psum = ctx.enter_context(tc.psum_pool(name="acc_psum", bufs=5))
+
+
+        b_rows = keep.tile([P, PACK, CHUNK], BF16)
+        b_by_plane = B.rearrange("(q t) (s r) -> t s q r", t=PACK, s=N_CHUNKS)
+        for t in range(PACK):
+            nc.sync.dma_start(out=b_rows[:, t, :], in_=b_by_plane[t])
 
         a_rows = keep.tile([P, A_COLS], BF16)
         a_by_quarter = A.rearrange("i (h r) -> (i h) r", h=A_SPLIT)
-        b_planes = keep.tile([P, PACK, R], BF16)
-        b_by_plane = B.rearrange("(q t) r -> t q r", t=PACK)
+        for n in range(A_COLS // CHUNK):
+            cols = slice(n * CHUNK, (n + 1) * CHUNK)
+            nc.sync.dma_start(out=a_rows[:, cols], in_=a_by_quarter[:, cols])
+
         g_rows = keep.tile([P, PASSES, PACK, N3], BF16)
         g_by_pass = grad_out.rearrange("i j k -> (i j) k").rearrange(
             "(c p t) k -> c p t k", c=PASSES, t=PACK
         )
-
-        def load_a(n):
-            cols = slice(n * CHUNK, (n + 1) * CHUNK)
-            nc.sync.dma_start(out=a_rows[:, cols], in_=a_by_quarter[:, cols])
-
-        def load_b(n):
-            cols = slice(n * CHUNK, (n + 1) * CHUNK)
-            for t in range(PACK):
-                nc.sync.dma_start(
-                    out=b_planes[:, t, cols],
-                    in_=b_by_plane[t, :, cols].unsqueeze(0).to_broadcast([P // Q, Q, CHUNK]),
-                )
-
-        load_a(0)
-        load_b(0)
         for c in range(PASSES):
             nc.sync.dma_start(out=g_rows[:, c], in_=g_by_pass[c])
-        for n in range(1, N_CHUNKS):
-            if n * CHUNK < A_COLS:
-                load_a(n)
-            load_b(n)
 
         ident = keep.tile([P, P], BF16)
         make_identity(nc, ident[:])
@@ -106,44 +86,69 @@ def tile_recon_loss_pa_kernel(tc, X, A, B, C, grad_out, out):
             .to_broadcast([P, A_SPLIT, N1, Q]),
         )
 
+        b_packed = keep.tile([P, CHUNK, PACK], BF16)
+        regroup_on_vector(nc, b_packed[:], b_rows[:])
+        nc.sync.dma_start(
+            out=out[0 : 2 * P, R - CHUNK : R].rearrange("(h p) w -> p h w", h=2),
+            in_=b_packed[:]
+            .rearrange("p r t -> p (r t)")
+            .bitcast(F32)
+            .rearrange("p (h w) -> p h w", h=2),
+        )
+        b_grouped = keep.tile([P, N_CHUNKS, CHUNK * PACK], BF16)
+
+        def load_b(n):
+            words = b_grouped[:, n, :].bitcast(F32)
+            for h in range(2):
+                nc.sync.dma_start(
+                    out=words[:, h * CHUNK : (h + 1) * CHUNK],
+                    in_=out[h * P + n * Q : h * P + (n + 1) * Q, R - CHUNK : R]
+                    .unsqueeze(0)
+                    .to_broadcast([P // Q, Q, CHUNK]),
+                )
+
+        for n in range(B_AHEAD):
+            load_b(n)
+
         g_grouped = keep.tile([P, PASSES, N3, PACK], BF16, align_bytes=64)
         g_codes = keep.tile([P, PASSES, N3], U32, align_bytes=64)
         g_scales = keep.tile([P, PASSES, N3], U8, align_bytes=64)
 
-        def prepare_g():
-            regroup_on_vector(nc, g_grouped[:, 0], g_rows[:, 0])
-            regroup_on_scalar(nc, g_grouped[:, 1], g_rows[:, 1])
-
-        def quantise_g():
-            nc.vector.quantize_mx(
-                out=g_codes[:].rearrange("p c k -> p (c k)").bitcast(E5M2_X4),
-                scales=g_scales[:].rearrange("p c k -> p (c k)"),
-                in_=g_grouped[:].rearrange("p c k t -> p (c k t)"),
-            )
-
         def spread_a(n):
             h, a_col = divmod(n * CHUNK, A_COLS)
-            a_spread = a_psum.tile([P, PASSES, CHUNK], BF16)
-            for c in range(PASSES):
+            twice = a0_psum.tile([P, CHUNK, 2], BF16)
+            for v in range(2):
                 nc.tensor.matmul(
-                    out=a_spread[:, c, :],
-                    lhsT=spread[:, h, c, :],
-                    rhs=a_rows[:, a_col : a_col + CHUNK],
+                    out=twice[:, v * HALF : (v + 1) * HALF, :],
+                    lhsT=spread[:, h, 0, :],
+                    rhs=a_rows[:, a_col + v * HALF : a_col + (v + 1) * HALF]
+                    .unsqueeze(2)
+                    .to_broadcast([P, HALF, 2]),
                     start=True,
                     stop=True,
                 )
-            return a_spread
+            once = a1_psum.tile([P, CHUNK], BF16)
+            nc.tensor.matmul(
+                out=once[:],
+                lhsT=spread[:, h, 1, :],
+                rhs=a_rows[:, a_col : a_col + CHUNK],
+                start=True,
+                stop=True,
+            )
+            return twice, once
 
-        def products(n, a_spread):
-            shape = [P, PASSES, PACK, CHUNK]
-            planar = work.tile(shape, BF16)
+        def double_a(once):
+            twice = work.tile([P, CHUNK, 2], BF16, name="twice_sb")
+            nc.scalar.copy(out=twice[:], in_=once[:].unsqueeze(2).to_broadcast([P, CHUNK, 2]))
+            return twice
+
+        def products(n, c, twice, grouped):
             nc.vector.tensor_tensor(
-                out=planar[:],
-                in0=b_planes[:, :, n * CHUNK : (n + 1) * CHUNK].unsqueeze(1).to_broadcast(shape),
-                in1=a_spread[:].unsqueeze(2).to_broadcast(shape),
+                out=grouped[:, c].rearrange("p r (u e) -> p r u e", e=2),
+                in0=b_grouped[:, n, :].rearrange("p (r u e) -> p r u e", u=2, e=2),
+                in1=twice[:].unsqueeze(2).to_broadcast([P, CHUNK, 2, 2]),
                 op=mybir.AluOpType.mult,
             )
-            return planar
 
         def quantise(grouped):
             codes = work.tile([P, PASSES, CHUNK], U32, align_bytes=64)
@@ -180,26 +185,36 @@ def tile_recon_loss_pa_kernel(tc, X, A, B, C, grad_out, out):
                 out=out[m * P : (m + 1) * P, n * CHUNK : (n + 1) * CHUNK], in_=result[:]
             )
 
-        a_spread = {0: spread_a(0)}
+        a_twice = {}
+        for n in range(2):
+            twice, once = spread_a(n)
+            a_twice[n] = (twice, double_a(once))
+
+        regroup_on_vector(nc, g_grouped[:, 0], g_rows[:, 0])
+        regroup_on_scalar(nc, g_grouped[:, 1], g_rows[:, 1])
+        nc.vector.quantize_mx(
+            out=g_codes[:].rearrange("p c k -> p (c k)").bitcast(E5M2_X4),
+            scales=g_scales[:].rearrange("p c k -> p (c k)"),
+            in_=g_grouped[:].rearrange("p c k t -> p (c k t)"),
+        )
+
         grouped = {}
-        banks = {}
-        for n in range(N_CHUNKS + 3):
-            if n + 1 < N_CHUNKS:
-                a_spread[n + 1] = spread_a(n + 1)
+        for n in range(N_CHUNKS + 1):
+            if n + B_AHEAD < N_CHUNKS:
+                load_b(n + B_AHEAD)
             if n < N_CHUNKS:
-                planar = products(n, a_spread[n])
-                grouped[n] = work.tile([P, PASSES, CHUNK, PACK], BF16, align_bytes=64, name="grouped")
-                regroup_on_gpsimd(nc, grouped[n][:, 0], planar[:, 0])
-                regroup_on_scalar(nc, grouped[n][:, 1], planar[:, 1])
-            if n == 0:
-                prepare_g()
-            if n == 2:
-                quantise_g()
-            if 0 <= n - 2 < N_CHUNKS:
-                codes, scales = quantise(grouped[n - 2])
-            if 0 <= n - 3 < N_CHUNKS:
-                store(n - 3, M_TILES - 1, nc.vector.tensor_copy, banks[n - 3][M_TILES - 1])
-            if 0 <= n - 2 < N_CHUNKS:
-                banks[n - 2] = multiply(codes, scales)
-                for m in range(M_TILES - 1):
-                    store(n - 2, m, nc.scalar.copy, banks[n - 2][m])
+                grouped[n] = work.tile(
+                    [P, PASSES, CHUNK, PACK], BF16, align_bytes=64, name="grouped"
+                )
+                products(n, 0, a_twice[n][0], grouped[n])
+            if n + 2 < N_CHUNKS:
+                twice, once = spread_a(n + 2)
+                a_twice[n + 2] = (twice, double_a(once))
+            if n < N_CHUNKS:
+                products(n, 1, a_twice[n][1], grouped[n])
+            if n >= 1:
+                codes, scales = quantise(grouped[n - 1])
+                banks = multiply(codes, scales)
+                for m in range(M_TILES):
+                    last = n == N_CHUNKS and m % 2 == 1
+                    store(n - 1, m, nc.vector.tensor_copy if last else nc.scalar.copy, banks[m])

@@ -40,6 +40,17 @@ def regroup_on_vector(nc, grouped, planar):
     nc.vector.tensor_copy(out=dst, in_=src)
 
 
+def regroup_on_gpsimd(nc, grouped, planar):
+    nc.gpsimd.tensor_scalar(
+        out=grouped,
+        in0=planar.rearrange("p t w -> p w t"),
+        scalar1=1.0,
+        scalar2=0.0,
+        op0=mybir.AluOpType.mult,
+        op1=mybir.AluOpType.add,
+    )
+
+
 def regroup_on_scalar(nc, grouped, planar):
     dst, src = regroup_views(grouped, planar)
     nc.scalar.copy(out=dst, in_=src)
@@ -64,9 +75,20 @@ def tile_recon_loss_pa_kernel(tc, X, A, B, C, grad_out, out):
 
         a_rows = keep.tile([P, A_COLS], BF16)
         a_by_quarter = A.rearrange("i (h r) -> (i h) r", h=A_SPLIT)
-        for n in range(A_COLS // CHUNK):
+
+        def load_a(n):
             cols = slice(n * CHUNK, (n + 1) * CHUNK)
             nc.sync.dma_start(out=a_rows[:, cols], in_=a_by_quarter[:, cols])
+
+        load_a(0)
+        b_planes = keep.tile([P, PACK, CHUNK], BF16)
+        b_first = B.rearrange("(q t) r -> t q r", t=PACK)
+        for t in range(PACK):
+            nc.sync.dma_start(
+                out=b_planes[:, t, :],
+                in_=b_first[t, :, 0:CHUNK].unsqueeze(0).to_broadcast([P // Q, Q, CHUNK]),
+            )
+        load_a(1)
 
         g_rows = keep.tile([P, PASSES, PACK, N3], BF16)
         g_by_pass = grad_out.rearrange("i j k -> (i j) k").rearrange(
@@ -74,6 +96,8 @@ def tile_recon_loss_pa_kernel(tc, X, A, B, C, grad_out, out):
         )
         for c in range(PASSES):
             nc.sync.dma_start(out=g_rows[:, c], in_=g_by_pass[c])
+        load_a(2)
+        load_a(3)
 
         ident = keep.tile([P, P], BF16)
         make_identity(nc, ident[:])
@@ -107,7 +131,7 @@ def tile_recon_loss_pa_kernel(tc, X, A, B, C, grad_out, out):
                     .to_broadcast([P // Q, Q, CHUNK]),
                 )
 
-        for n in range(B_AHEAD):
+        for n in range(1, B_AHEAD):
             load_b(n)
 
         g_grouped = keep.tile([P, PASSES, N3, PACK], BF16, align_bytes=64)
@@ -136,6 +160,19 @@ def tile_recon_loss_pa_kernel(tc, X, A, B, C, grad_out, out):
                 stop=True,
             )
             return twice, once
+
+        def spread_a_once(n):
+            h, a_col = divmod(n * CHUNK, A_COLS)
+            twice = a0_psum.tile([P, PASSES, CHUNK], BF16)
+            for c in range(PASSES):
+                nc.tensor.matmul(
+                    out=twice[:, c, :],
+                    lhsT=spread[:, h, c, :],
+                    rhs=a_rows[:, a_col : a_col + CHUNK],
+                    start=True,
+                    stop=True,
+                )
+            return twice
 
         def double_a(once):
             twice = work.tile([P, CHUNK, 2], BF16, name="twice_sb")
@@ -186,17 +223,10 @@ def tile_recon_loss_pa_kernel(tc, X, A, B, C, grad_out, out):
             )
 
         a_twice = {}
-        for n in range(2):
-            twice, once = spread_a(n)
-            a_twice[n] = (twice, double_a(once))
-
-        regroup_on_vector(nc, g_grouped[:, 0], g_rows[:, 0])
+        a_first = spread_a_once(0)
+        twice, once = spread_a(1)
+        a_twice[1] = (twice, double_a(once))
         regroup_on_scalar(nc, g_grouped[:, 1], g_rows[:, 1])
-        nc.vector.quantize_mx(
-            out=g_codes[:].rearrange("p c k -> p (c k)").bitcast(E5M2_X4),
-            scales=g_scales[:].rearrange("p c k -> p (c k)"),
-            in_=g_grouped[:].rearrange("p c k t -> p (c k t)"),
-        )
 
         grouped = {}
         for n in range(N_CHUNKS + 1):
@@ -206,11 +236,30 @@ def tile_recon_loss_pa_kernel(tc, X, A, B, C, grad_out, out):
                 grouped[n] = work.tile(
                     [P, PASSES, CHUNK, PACK], BF16, align_bytes=64, name="grouped"
                 )
-                products(n, 0, a_twice[n][0], grouped[n])
+                if n == 0:
+                    shape = [P, PASSES, PACK, CHUNK]
+                    planar = keep.tile(shape, BF16)
+                    nc.vector.tensor_tensor(
+                        out=planar[:],
+                        in0=b_planes[:].unsqueeze(1).to_broadcast(shape),
+                        in1=a_first[:].unsqueeze(2).to_broadcast(shape),
+                        op=mybir.AluOpType.mult,
+                    )
+                else:
+                    products(n, 0, a_twice[n][0], grouped[n])
             if n + 2 < N_CHUNKS:
                 twice, once = spread_a(n + 2)
                 a_twice[n + 2] = (twice, double_a(once))
-            if n < N_CHUNKS:
+            if n == 0:
+                regroup_on_gpsimd(nc, grouped[0][:, 0], planar[:, 0])
+                regroup_on_scalar(nc, grouped[0][:, 1], planar[:, 1])
+                regroup_on_vector(nc, g_grouped[:, 0], g_rows[:, 0])
+                nc.vector.quantize_mx(
+                    out=g_codes[:].rearrange("p c k -> p (c k)").bitcast(E5M2_X4),
+                    scales=g_scales[:].rearrange("p c k -> p (c k)"),
+                    in_=g_grouped[:].rearrange("p c k t -> p (c k t)"),
+                )
+            elif n < N_CHUNKS:
                 products(n, 1, a_twice[n][1], grouped[n])
             if n >= 1:
                 codes, scales = quantise(grouped[n - 1])

@@ -23,6 +23,7 @@ A_SPLIT = P // N1
 A_COLS = R // A_SPLIT
 HALF = CHUNK // 2
 B_AHEAD = 6
+BOTH_EVERY = 4
 
 FLOPS = 2 * N1 * N2 * N3 * R
 BYTES = 2 * (N1 * R + N2 * R + N1 * N2 * N3) + 4 * N3 * R
@@ -63,9 +64,9 @@ def tile_recon_loss_pa_kernel(tc, X, A, B, C, grad_out, out):
         keep = ctx.enter_context(tc.tile_pool(name="keep", bufs=1))
         work = ctx.enter_context(tc.tile_pool(name="work", bufs=3))
         stage = ctx.enter_context(tc.tile_pool(name="stage", bufs=12))
-        a0_psum = ctx.enter_context(tc.psum_pool(name="a0_psum", bufs=2))
+        a0_psum = ctx.enter_context(tc.psum_pool(name="a0_psum", bufs=3))
         a1_psum = ctx.enter_context(tc.psum_pool(name="a1_psum", bufs=1))
-        acc_psum = ctx.enter_context(tc.psum_pool(name="acc_psum", bufs=5))
+        acc_psum = ctx.enter_context(tc.psum_pool(name="acc_psum", bufs=4))
 
 
         b_rows = keep.tile([P, PACK, CHUNK], BF16)
@@ -138,19 +139,26 @@ def tile_recon_loss_pa_kernel(tc, X, A, B, C, grad_out, out):
         g_codes = keep.tile([P, PASSES, N3], U32, align_bytes=64)
         g_scales = keep.tile([P, PASSES, N3], U8, align_bytes=64)
 
-        def spread_a(n):
+        def spread_twice(n, c):
             h, a_col = divmod(n * CHUNK, A_COLS)
             twice = a0_psum.tile([P, CHUNK, 2], BF16)
             for v in range(2):
                 nc.tensor.matmul(
                     out=twice[:, v * HALF : (v + 1) * HALF, :],
-                    lhsT=spread[:, h, 0, :],
+                    lhsT=spread[:, h, c, :],
                     rhs=a_rows[:, a_col + v * HALF : a_col + (v + 1) * HALF]
                     .unsqueeze(2)
                     .to_broadcast([P, HALF, 2]),
                     start=True,
                     stop=True,
                 )
+            return twice
+
+        def spread_a(n):
+            first = spread_twice(n, 0)
+            if n % BOTH_EVERY == 2:
+                return first, spread_twice(n, 1)
+            h, a_col = divmod(n * CHUNK, A_COLS)
             once = a1_psum.tile([P, CHUNK], BF16)
             nc.tensor.matmul(
                 out=once[:],
@@ -159,7 +167,7 @@ def tile_recon_loss_pa_kernel(tc, X, A, B, C, grad_out, out):
                 start=True,
                 stop=True,
             )
-            return twice, once
+            return first, double_a(once)
 
         def spread_a_once(n):
             h, a_col = divmod(n * CHUNK, A_COLS)
@@ -224,8 +232,7 @@ def tile_recon_loss_pa_kernel(tc, X, A, B, C, grad_out, out):
 
         a_twice = {}
         a_first = spread_a_once(0)
-        twice, once = spread_a(1)
-        a_twice[1] = (twice, double_a(once))
+        a_twice[1] = spread_a(1)
         regroup_on_scalar(nc, g_grouped[:, 1], g_rows[:, 1])
 
         grouped = {}
@@ -248,8 +255,7 @@ def tile_recon_loss_pa_kernel(tc, X, A, B, C, grad_out, out):
                 else:
                     products(n, 0, a_twice[n][0], grouped[n])
             if n + 2 < N_CHUNKS:
-                twice, once = spread_a(n + 2)
-                a_twice[n + 2] = (twice, double_a(once))
+                a_twice[n + 2] = spread_a(n + 2)
             if n == 0:
                 regroup_on_gpsimd(nc, grouped[0][:, 0], planar[:, 0])
                 regroup_on_scalar(nc, grouped[0][:, 1], planar[:, 1])

@@ -23,7 +23,6 @@ A_SPLIT = P // N1
 A_COLS = R // A_SPLIT
 HALF = CHUNK // 2
 B_AHEAD = 6
-BOTH_EVERY = 4
 
 FLOPS = 2 * N1 * N2 * N3 * R
 BYTES = 2 * (N1 * R + N2 * R + N1 * N2 * N3) + 4 * N3 * R
@@ -39,17 +38,6 @@ def regroup_views(grouped, planar):
 def regroup_on_vector(nc, grouped, planar):
     dst, src = regroup_views(grouped, planar)
     nc.vector.tensor_copy(out=dst, in_=src)
-
-
-def regroup_on_gpsimd(nc, grouped, planar):
-    nc.gpsimd.tensor_scalar(
-        out=grouped,
-        in0=planar.rearrange("p t w -> p w t"),
-        scalar1=1.0,
-        scalar2=0.0,
-        op0=mybir.AluOpType.mult,
-        op1=mybir.AluOpType.add,
-    )
 
 
 def regroup_on_scalar(nc, grouped, planar):
@@ -82,13 +70,6 @@ def tile_recon_loss_pa_kernel(tc, X, A, B, C, grad_out, out):
             nc.sync.dma_start(out=a_rows[:, cols], in_=a_by_quarter[:, cols])
 
         load_a(0)
-        b_planes = keep.tile([P, PACK, CHUNK], BF16)
-        b_first = B.rearrange("(q t) r -> t q r", t=PACK)
-        for t in range(PACK):
-            nc.sync.dma_start(
-                out=b_planes[:, t, :],
-                in_=b_first[t, :, 0:CHUNK].unsqueeze(0).to_broadcast([P // Q, Q, CHUNK]),
-            )
         load_a(1)
 
         g_rows = keep.tile([P, PASSES, PACK, N3], BF16)
@@ -109,6 +90,11 @@ def tile_recon_loss_pa_kernel(tc, X, A, B, C, grad_out, out):
             .rearrange("k (m h) -> k h m", h=A_SPLIT)
             .unsqueeze(3)
             .to_broadcast([P, A_SPLIT, N1, Q]),
+        )
+        repeat = keep.tile([P, P], BF16)
+        nc.vector.tensor_copy(
+            out=repeat[:].rearrange("k (g q) -> k g q", q=Q),
+            in_=ident[:, 0:Q].unsqueeze(1).to_broadcast([P, P // Q, Q]),
         )
 
         b_packed = keep.tile([P, CHUNK, PACK], BF16)
@@ -155,45 +141,35 @@ def tile_recon_loss_pa_kernel(tc, X, A, B, C, grad_out, out):
             return twice
 
         def spread_a(n):
-            first = spread_twice(n, 0)
-            if n % BOTH_EVERY == 2:
-                return first, spread_twice(n, 1)
+            return spread_twice(n, 0), spread_once(n, 1)
+
+        def spread_once(n, c):
             h, a_col = divmod(n * CHUNK, A_COLS)
             once = a1_psum.tile([P, CHUNK], BF16)
             nc.tensor.matmul(
                 out=once[:],
-                lhsT=spread[:, h, 1, :],
+                lhsT=spread[:, h, c, :],
                 rhs=a_rows[:, a_col : a_col + CHUNK],
                 start=True,
                 stop=True,
             )
-            return first, double_a(once)
-
-        def spread_a_once(n):
-            h, a_col = divmod(n * CHUNK, A_COLS)
-            twice = a0_psum.tile([P, PASSES, CHUNK], BF16)
-            for c in range(PASSES):
-                nc.tensor.matmul(
-                    out=twice[:, c, :],
-                    lhsT=spread[:, h, c, :],
-                    rhs=a_rows[:, a_col : a_col + CHUNK],
-                    start=True,
-                    stop=True,
-                )
-            return twice
+            return double_a(once)
 
         def double_a(once):
             twice = work.tile([P, CHUNK, 2], BF16, name="twice_sb")
             nc.scalar.copy(out=twice[:], in_=once[:].unsqueeze(2).to_broadcast([P, CHUNK, 2]))
             return twice
 
-        def products(n, c, twice, grouped):
+        def products_of(b_part, c, twice, grouped, first, last):
             nc.vector.tensor_tensor(
-                out=grouped[:, c].rearrange("p r (u e) -> p r u e", e=2),
-                in0=b_grouped[:, n, :].rearrange("p (r u e) -> p r u e", u=2, e=2),
-                in1=twice[:].unsqueeze(2).to_broadcast([P, CHUNK, 2, 2]),
+                out=grouped[:, c, first:last].rearrange("p r (u e) -> p r u e", e=2),
+                in0=b_part.rearrange("p (r u e) -> p r u e", u=2, e=2),
+                in1=twice[:, first:last].unsqueeze(2).to_broadcast([P, last - first, 2, 2]),
                 op=mybir.AluOpType.mult,
             )
+
+        def products(n, c, twice, grouped):
+            products_of(b_grouped[:, n, :], c, twice, grouped, 0, CHUNK)
 
         def quantise(grouped):
             codes = work.tile([P, PASSES, CHUNK], U32, align_bytes=64)
@@ -209,7 +185,7 @@ def tile_recon_loss_pa_kernel(tc, X, A, B, C, grad_out, out):
             banks = []
             for m in range(M_TILES):
                 rows = slice(m * P, (m + 1) * P)
-                acc = acc_psum.tile([P, CHUNK], F32)
+                acc = acc_psum.tile([P, CHUNK], F32, name="acc")
                 for c in range(PASSES):
                     nc.tensor.matmul_mx(
                         out=acc[:],
@@ -231,9 +207,23 @@ def tile_recon_loss_pa_kernel(tc, X, A, B, C, grad_out, out):
             )
 
         a_twice = {}
-        a_first = spread_a_once(0)
-        a_twice[1] = spread_a(1)
+        a_twice[0] = spread_once(0, 0), spread_once(0, 1)
+        b_flat = b_packed[:].rearrange("p r t -> p (r t)")
+        b_first = []
+        for v in range(2):
+            bank = acc_psum.tile([P, HALF * PACK], BF16, name="acc")
+            for w in range(2):
+                nc.tensor.matmul(
+                    out=bank[:, w * CHUNK : (w + 1) * CHUNK],
+                    lhsT=repeat[:],
+                    rhs=b_flat[:, (2 * v + w) * CHUNK : (2 * v + w + 1) * CHUNK],
+                    start=True,
+                    stop=True,
+                )
+            b_first.append(bank)
         regroup_on_scalar(nc, g_grouped[:, 1], g_rows[:, 1])
+        regroup_on_vector(nc, g_grouped[:, 0], g_rows[:, 0])
+        a_twice[1] = spread_a(1)
 
         grouped = {}
         for n in range(N_CHUNKS + 1):
@@ -244,22 +234,16 @@ def tile_recon_loss_pa_kernel(tc, X, A, B, C, grad_out, out):
                     [P, PASSES, CHUNK, PACK], BF16, align_bytes=64, name="grouped"
                 )
                 if n == 0:
-                    shape = [P, PASSES, PACK, CHUNK]
-                    planar = keep.tile(shape, BF16)
-                    nc.vector.tensor_tensor(
-                        out=planar[:],
-                        in0=b_planes[:].unsqueeze(1).to_broadcast(shape),
-                        in1=a_first[:].unsqueeze(2).to_broadcast(shape),
-                        op=mybir.AluOpType.mult,
-                    )
+                    for c in range(PASSES):
+                        for v in range(2):
+                            products_of(
+                                b_first[v][:], c, a_twice[0][c], grouped[0], v * HALF, (v + 1) * HALF
+                            )
                 else:
                     products(n, 0, a_twice[n][0], grouped[n])
             if n + 2 < N_CHUNKS:
                 a_twice[n + 2] = spread_a(n + 2)
             if n == 0:
-                regroup_on_gpsimd(nc, grouped[0][:, 0], planar[:, 0])
-                regroup_on_scalar(nc, grouped[0][:, 1], planar[:, 1])
-                regroup_on_vector(nc, g_grouped[:, 0], g_rows[:, 0])
                 nc.vector.quantize_mx(
                     out=g_codes[:].rearrange("p c k -> p (c k)").bitcast(E5M2_X4),
                     scales=g_scales[:].rearrange("p c k -> p (c k)"),

@@ -23,6 +23,7 @@ A_SPLIT = P // N1
 A_COLS = R // A_SPLIT
 HALF = CHUNK // 2
 B_AHEAD = 6
+G_COLS = 64
 
 FLOPS = 2 * N1 * N2 * N3 * R
 BYTES = 2 * (N1 * R + N2 * R + N1 * N2 * N3) + 4 * N3 * R
@@ -52,8 +53,8 @@ def tile_recon_loss_pa_kernel(tc, X, A, B, C, grad_out, out):
         keep = ctx.enter_context(tc.tile_pool(name="keep", bufs=1))
         work = ctx.enter_context(tc.tile_pool(name="work", bufs=3))
         stage = ctx.enter_context(tc.tile_pool(name="stage", bufs=12))
-        a0_psum = ctx.enter_context(tc.psum_pool(name="a0_psum", bufs=3))
-        a1_psum = ctx.enter_context(tc.psum_pool(name="a1_psum", bufs=1))
+        a0_psum = ctx.enter_context(tc.psum_pool(name="a0_psum", bufs=2))
+        a1_psum = ctx.enter_context(tc.psum_pool(name="a1_psum", bufs=2))
         acc_psum = ctx.enter_context(tc.psum_pool(name="acc_psum", bufs=4))
 
 
@@ -160,16 +161,17 @@ def tile_recon_loss_pa_kernel(tc, X, A, B, C, grad_out, out):
             nc.scalar.copy(out=twice[:], in_=once[:].unsqueeze(2).to_broadcast([P, CHUNK, 2]))
             return twice
 
-        def products_of(b_part, c, twice, grouped, first, last):
-            nc.vector.tensor_tensor(
+        def products_of(engine, b_part, c, twice, grouped, first, last):
+            engine.tensor_tensor(
                 out=grouped[:, c, first:last].rearrange("p r (u e) -> p r u e", e=2),
                 in0=b_part.rearrange("p (r u e) -> p r u e", u=2, e=2),
                 in1=twice[:, first:last].unsqueeze(2).to_broadcast([P, last - first, 2, 2]),
                 op=mybir.AluOpType.mult,
             )
 
-        def products(n, c, twice, grouped):
-            products_of(b_grouped[:, n, :], c, twice, grouped, 0, CHUNK)
+        def products(engine, n, c, twice, grouped, first, last):
+            b_part = b_grouped[:, n, first * PACK : last * PACK]
+            products_of(engine, b_part, c, twice, grouped, first, last)
 
         def quantise(grouped):
             codes = work.tile([P, PASSES, CHUNK], U32, align_bytes=64)
@@ -237,10 +239,17 @@ def tile_recon_loss_pa_kernel(tc, X, A, B, C, grad_out, out):
                     for c in range(PASSES):
                         for v in range(2):
                             products_of(
-                                b_first[v][:], c, a_twice[0][c], grouped[0], v * HALF, (v + 1) * HALF
+                                nc.vector,
+                                b_first[v][:],
+                                c,
+                                a_twice[0][c],
+                                grouped[0],
+                                v * HALF,
+                                (v + 1) * HALF,
                             )
                 else:
-                    products(n, 0, a_twice[n][0], grouped[n])
+                    products(nc.gpsimd, n, 1, a_twice[n][1], grouped[n], CHUNK - G_COLS, CHUNK)
+                    products(nc.vector, n, 0, a_twice[n][0], grouped[n], 0, CHUNK)
             if n + 2 < N_CHUNKS:
                 a_twice[n + 2] = spread_a(n + 2)
             if n == 0:
@@ -249,10 +258,12 @@ def tile_recon_loss_pa_kernel(tc, X, A, B, C, grad_out, out):
                     scales=g_scales[:].rearrange("p c k -> p (c k)"),
                     in_=g_grouped[:].rearrange("p c k t -> p (c k t)"),
                 )
-            elif n < N_CHUNKS:
-                products(n, 1, a_twice[n][1], grouped[n])
+            elif n < N_CHUNKS - 1:
+                products(nc.vector, n, 1, a_twice[n][1], grouped[n], 0, CHUNK - G_COLS)
             if n >= 1:
                 codes, scales = quantise(grouped[n - 1])
+                if n == N_CHUNKS - 1:
+                    products(nc.vector, n, 1, a_twice[n][1], grouped[n], 0, CHUNK - G_COLS)
                 banks = multiply(codes, scales)
                 for m in range(M_TILES):
                     last = n == N_CHUNKS and m % 2 == 1

@@ -24,6 +24,8 @@ A_COLS = R // A_SPLIT
 HALF = CHUNK // 2
 B_AHEAD = 6
 G_COLS = 64
+FIRST = 2
+ALL_ON_SCALAR = 5
 
 FLOPS = 2 * N1 * N2 * N3 * R
 BYTES = 2 * (N1 * R + N2 * R + N1 * N2 * N3) + 4 * N3 * R
@@ -41,9 +43,15 @@ def regroup_on_vector(nc, grouped, planar):
     nc.vector.tensor_copy(out=dst, in_=src)
 
 
-def regroup_on_scalar(nc, grouped, planar):
-    dst, src = regroup_views(grouped, planar)
-    nc.scalar.copy(out=dst, in_=src)
+def regroup_on_gpsimd(nc, grouped, planar):
+    nc.gpsimd.tensor_scalar(
+        out=grouped,
+        in0=planar.rearrange("p t w -> p w t"),
+        scalar1=1.0,
+        scalar2=0.0,
+        op0=mybir.AluOpType.mult,
+        op1=mybir.AluOpType.add,
+    )
 
 
 def tile_recon_loss_pa_kernel(tc, X, A, B, C, grad_out, out):
@@ -52,6 +60,7 @@ def tile_recon_loss_pa_kernel(tc, X, A, B, C, grad_out, out):
         ctx.enter_context(tc.manual_schedule())
         keep = ctx.enter_context(tc.tile_pool(name="keep", bufs=1))
         work = ctx.enter_context(tc.tile_pool(name="work", bufs=3))
+        pairs = ctx.enter_context(tc.tile_pool(name="pairs", bufs=8))
         stage = ctx.enter_context(tc.tile_pool(name="stage", bufs=12))
         a0_psum = ctx.enter_context(tc.psum_pool(name="a0_psum", bufs=2))
         a1_psum = ctx.enter_context(tc.psum_pool(name="a1_psum", bufs=2))
@@ -92,10 +101,13 @@ def tile_recon_loss_pa_kernel(tc, X, A, B, C, grad_out, out):
             .unsqueeze(3)
             .to_broadcast([P, A_SPLIT, N1, Q]),
         )
-        repeat = keep.tile([P, P], BF16)
+        repeat = keep.tile([P, FIRST, P], BF16)
         nc.vector.tensor_copy(
-            out=repeat[:].rearrange("k (g q) -> k g q", q=Q),
-            in_=ident[:, 0:Q].unsqueeze(1).to_broadcast([P, P // Q, Q]),
+            out=repeat[:].rearrange("k s (g q) -> k s g q", q=Q),
+            in_=ident[:, 0 : FIRST * Q]
+            .rearrange("k (s q) -> k s q", q=Q)
+            .unsqueeze(2)
+            .to_broadcast([P, FIRST, P // Q, Q]),
         )
 
         b_packed = keep.tile([P, CHUNK, PACK], BF16)
@@ -119,7 +131,7 @@ def tile_recon_loss_pa_kernel(tc, X, A, B, C, grad_out, out):
                     .to_broadcast([P // Q, Q, CHUNK]),
                 )
 
-        for n in range(1, B_AHEAD):
+        for n in range(FIRST, B_AHEAD):
             load_b(n)
 
         g_grouped = keep.tile([P, PASSES, N3, PACK], BF16, align_bytes=64)
@@ -142,7 +154,12 @@ def tile_recon_loss_pa_kernel(tc, X, A, B, C, grad_out, out):
             return twice
 
         def spread_a(n):
+            if all_in_sbuf(n):
+                return spread_once(n, 0), spread_once(n, 1)
             return spread_twice(n, 0), spread_once(n, 1)
+
+        def all_in_sbuf(n):
+            return n < ALL_ON_SCALAR
 
         def spread_once(n, c):
             h, a_col = divmod(n * CHUNK, A_COLS)
@@ -157,7 +174,7 @@ def tile_recon_loss_pa_kernel(tc, X, A, B, C, grad_out, out):
             return double_a(once)
 
         def double_a(once):
-            twice = work.tile([P, CHUNK, 2], BF16, name="twice_sb")
+            twice = pairs.tile([P, CHUNK, 2], BF16, name="twice_sb")
             nc.scalar.copy(out=twice[:], in_=once[:].unsqueeze(2).to_broadcast([P, CHUNK, 2]))
             return twice
 
@@ -209,23 +226,23 @@ def tile_recon_loss_pa_kernel(tc, X, A, B, C, grad_out, out):
             )
 
         a_twice = {}
-        a_twice[0] = spread_once(0, 0), spread_once(0, 1)
         b_flat = b_packed[:].rearrange("p r t -> p (r t)")
-        b_first = []
-        for v in range(2):
-            bank = acc_psum.tile([P, HALF * PACK], BF16, name="acc")
-            for w in range(2):
-                nc.tensor.matmul(
-                    out=bank[:, w * CHUNK : (w + 1) * CHUNK],
-                    lhsT=repeat[:],
-                    rhs=b_flat[:, (2 * v + w) * CHUNK : (2 * v + w + 1) * CHUNK],
-                    start=True,
-                    stop=True,
-                )
-            b_first.append(bank)
-        regroup_on_scalar(nc, g_grouped[:, 1], g_rows[:, 1])
+        b_first = {}
+        for n in range(FIRST):
+            a_twice[n] = spread_a(n)
+            for v in range(2):
+                bank = acc_psum.tile([P, HALF * PACK], BF16, name="acc")
+                for w in range(2):
+                    nc.tensor.matmul(
+                        out=bank[:, w * CHUNK : (w + 1) * CHUNK],
+                        lhsT=repeat[:, n, :],
+                        rhs=b_flat[:, (2 * v + w) * CHUNK : (2 * v + w + 1) * CHUNK],
+                        start=True,
+                        stop=True,
+                    )
+                b_first[n, v] = bank
+        regroup_on_gpsimd(nc, g_grouped[:, 1], g_rows[:, 1])
         regroup_on_vector(nc, g_grouped[:, 0], g_rows[:, 0])
-        a_twice[1] = spread_a(1)
 
         grouped = {}
         for n in range(N_CHUNKS + 1):
@@ -235,35 +252,37 @@ def tile_recon_loss_pa_kernel(tc, X, A, B, C, grad_out, out):
                 grouped[n] = work.tile(
                     [P, PASSES, CHUNK, PACK], BF16, align_bytes=64, name="grouped"
                 )
-                if n == 0:
+                split = CHUNK if all_in_sbuf(n) else CHUNK - G_COLS
+                if n < FIRST:
                     for c in range(PASSES):
                         for v in range(2):
                             products_of(
                                 nc.vector,
-                                b_first[v][:],
+                                b_first[n, v][:],
                                 c,
-                                a_twice[0][c],
-                                grouped[0],
+                                a_twice[n][c],
+                                grouped[n],
                                 v * HALF,
                                 (v + 1) * HALF,
                             )
                 else:
-                    products(nc.gpsimd, n, 1, a_twice[n][1], grouped[n], CHUNK - G_COLS, CHUNK)
+                    if split < CHUNK:
+                        products(nc.gpsimd, n, 1, a_twice[n][1], grouped[n], split, CHUNK)
                     products(nc.vector, n, 0, a_twice[n][0], grouped[n], 0, CHUNK)
-            if n + 2 < N_CHUNKS:
+            if n + 2 < N_CHUNKS and n + 2 >= FIRST:
                 a_twice[n + 2] = spread_a(n + 2)
-            if n == 0:
+            if FIRST <= n < N_CHUNKS - 1:
+                products(nc.vector, n, 1, a_twice[n][1], grouped[n], 0, split)
+            if n == 1:
                 nc.vector.quantize_mx(
                     out=g_codes[:].rearrange("p c k -> p (c k)").bitcast(E5M2_X4),
                     scales=g_scales[:].rearrange("p c k -> p (c k)"),
                     in_=g_grouped[:].rearrange("p c k t -> p (c k t)"),
                 )
-            elif n < N_CHUNKS - 1:
-                products(nc.vector, n, 1, a_twice[n][1], grouped[n], 0, CHUNK - G_COLS)
             if n >= 1:
                 codes, scales = quantise(grouped[n - 1])
                 if n == N_CHUNKS - 1:
-                    products(nc.vector, n, 1, a_twice[n][1], grouped[n], 0, CHUNK - G_COLS)
+                    products(nc.vector, n, 1, a_twice[n][1], grouped[n], 0, split)
                 banks = multiply(codes, scales)
                 for m in range(M_TILES):
                     last = n == N_CHUNKS and m % 2 == 1

from contextlib import ExitStack

import concourse.mybir as mybir
from concourse.masks import make_identity

BF16 = mybir.dt.bfloat16
F32 = mybir.dt.float32
U32 = mybir.dt.uint32
U8 = mybir.dt.uint8
E4M3_X4 = mybir.dt.float8_e4m3fn_x4
E5M2_X4 = mybir.dt.float8_e5m2_x4

N1, N2, N3, R = 32, 32, 512, 8192
P = 128
PACK = 4
K_PASS = P * PACK
PASSES = (N1 * N2) // K_PASS
Q = N2 // PACK
M_TILES = N3 // P
CHUNK = 512
N_CHUNKS = R // CHUNK
A_SPLIT = P // N1
A_COLS = R // A_SPLIT
HALF = CHUNK // 2
B_AHEAD = 6
G_COLS = 64
FIRST = 2
ALL_ON_SCALAR = 5

FLOPS = 2 * N1 * N2 * N3 * R
BYTES = 2 * (N1 * R + N2 * R + N1 * N2 * N3) + 4 * N3 * R


def regroup_views(grouped, planar):
    return (
        grouped.rearrange("p (n i) t -> p n t i", i=4),
        planar.rearrange("p t (n i) -> p n t i", i=4),
    )


def regroup_on_vector(nc, grouped, planar):
    dst, src = regroup_views(grouped, planar)
    nc.vector.tensor_copy(out=dst, in_=src)


def regroup_on_gpsimd(nc, grouped, planar):
    nc.gpsimd.tensor_scalar(
        out=grouped,
        in0=planar.rearrange("p t w -> p w t"),
        scalar1=1.0,
        scalar2=0.0,
        op0=mybir.AluOpType.mult,
        op1=mybir.AluOpType.add,
    )


def tile_recon_loss_pa_kernel(tc, X, A, B, C, grad_out, out):
    nc = tc.nc
    with ExitStack() as ctx:
        ctx.enter_context(tc.manual_schedule())
        keep = ctx.enter_context(tc.tile_pool(name="keep", bufs=1))
        work = ctx.enter_context(tc.tile_pool(name="work", bufs=3))
        pairs = ctx.enter_context(tc.tile_pool(name="pairs", bufs=8))
        stage = ctx.enter_context(tc.tile_pool(name="stage", bufs=12))
        a0_psum = ctx.enter_context(tc.psum_pool(name="a0_psum", bufs=2))
        a1_psum = ctx.enter_context(tc.psum_pool(name="a1_psum", bufs=2))
        acc_psum = ctx.enter_context(tc.psum_pool(name="acc_psum", bufs=4))


        b_rows = keep.tile([P, PACK, CHUNK], BF16)
        b_by_plane = B.rearrange("(q t) (s r) -> t s q r", t=PACK, s=N_CHUNKS)
        for t in range(PACK):
            nc.sync.dma_start(out=b_rows[:, t, :], in_=b_by_plane[t])

        a_rows = keep.tile([P, A_COLS], BF16)
        a_by_quarter = A.rearrange("i (h r) -> (i h) r", h=A_SPLIT)

        def load_a(n):
            cols = slice(n * CHUNK, (n + 1) * CHUNK)
            nc.sync.dma_start(out=a_rows[:, cols], in_=a_by_quarter[:, cols])

        load_a(0)
        load_a(1)

        g_rows = keep.tile([P, PASSES, PACK, N3], BF16)
        g_by_pass = grad_out.rearrange("i j k -> (i j) k").rearrange(
            "(c p t) k -> c p t k", c=PASSES, t=PACK
        )
        for c in range(PASSES):
            nc.sync.dma_start(out=g_rows[:, c], in_=g_by_pass[c])
        load_a(2)
        load_a(3)

        ident = keep.tile([P, P], BF16)
        make_identity(nc, ident[:])
        spread = keep.tile([P, A_SPLIT, PASSES, P], BF16)
        nc.vector.tensor_copy(
            out=spread[:].rearrange("k h c (g e) -> k h (c g) e", e=Q),
            in_=ident[:]
            .rearrange("k (m h) -> k h m", h=A_SPLIT)
            .unsqueeze(3)
            .to_broadcast([P, A_SPLIT, N1, Q]),
        )
        repeat = keep.tile([P, FIRST, P], BF16)
        nc.vector.tensor_copy(
            out=repeat[:].rearrange("k s (g q) -> k s g q", q=Q),
            in_=ident[:, 0 : FIRST * Q]
            .rearrange("k (s q) -> k s q", q=Q)
            .unsqueeze(2)
            .to_broadcast([P, FIRST, P // Q, Q]),
        )

        b_packed = keep.tile([P, CHUNK, PACK], BF16)
        regroup_on_vector(nc, b_packed[:], b_rows[:])
        nc.sync.dma_start(
            out=out[0 : 2 * P, R - CHUNK : R].rearrange("(h p) w -> p h w", h=2),
            in_=b_packed[:]
            .rearrange("p r t -> p (r t)")
            .bitcast(F32)
            .rearrange("p (h w) -> p h w", h=2),
        )
        b_grouped = keep.tile([P, N_CHUNKS, CHUNK * PACK], BF16)

        def load_b(n):
            words = b_grouped[:, n, :].bitcast(F32)
            for h in range(2):
                nc.sync.dma_start(
                    out=words[:, h * CHUNK : (h + 1) * CHUNK],
                    in_=out[h * P + n * Q : h * P + (n + 1) * Q, R - CHUNK : R]
                    .unsqueeze(0)
                    .to_broadcast([P // Q, Q, CHUNK]),
                )

        for n in range(FIRST, B_AHEAD):
            load_b(n)

        g_grouped = keep.tile([P, PASSES, N3, PACK], BF16, align_bytes=64)
        g_codes = keep.tile([P, PASSES, N3], U32, align_bytes=64)
        g_scales = keep.tile([P, PASSES, N3], U8, align_bytes=64)

        def spread_twice(n, c):
            h, a_col = divmod(n * CHUNK, A_COLS)
            twice = a0_psum.tile([P, CHUNK, 2], BF16)
            for v in range(2):
                nc.tensor.matmul(
                    out=twice[:, v * HALF : (v + 1) * HALF, :],
                    lhsT=spread[:, h, c, :],
                    rhs=a_rows[:, a_col + v * HALF : a_col + (v + 1) * HALF]
                    .unsqueeze(2)
                    .to_broadcast([P, HALF, 2]),
                    start=True,
                    stop=True,
                )
            return twice

        def spread_a(n):
            if all_in_sbuf(n):
                return spread_once(n, 0), spread_once(n, 1)
            return spread_twice(n, 0), spread_once(n, 1)

        def all_in_sbuf(n):
            return n < ALL_ON_SCALAR

        def spread_once(n, c):
            h, a_col = divmod(n * CHUNK, A_COLS)
            once = a1_psum.tile([P, CHUNK], BF16)
            nc.tensor.matmul(
                out=once[:],
                lhsT=spread[:, h, c, :],
                rhs=a_rows[:, a_col : a_col + CHUNK],
                start=True,
                stop=True,
            )
            return double_a(once)

        def double_a(once):
            twice = pairs.tile([P, CHUNK, 2], BF16, name="twice_sb")
            nc.scalar.copy(out=twice[:], in_=once[:].unsqueeze(2).to_broadcast([P, CHUNK, 2]))
            return twice

        def products_of(engine, b_part, c, twice, grouped, first, last):
            engine.tensor_tensor(
                out=grouped[:, c, first:last].rearrange("p r (u e) -> p r u e", e=2),
                in0=b_part.rearrange("p (r u e) -> p r u e", u=2, e=2),
                in1=twice[:, first:last].unsqueeze(2).to_broadcast([P, last - first, 2, 2]),
                op=mybir.AluOpType.mult,
            )

        def products(engine, n, c, twice, grouped, first, last):
            b_part = b_grouped[:, n, first * PACK : last * PACK]
            products_of(engine, b_part, c, twice, grouped, first, last)

        def quantise(grouped):
            codes = work.tile([P, PASSES, CHUNK], U32, align_bytes=64)
            scales = work.tile([P, PASSES, CHUNK], U8, align_bytes=64)
            nc.vector.quantize_mx(
                out=codes[:].rearrange("p c r -> p (c r)").bitcast(E4M3_X4),
                scales=scales[:].rearrange("p c r -> p (c r)"),
                in_=grouped[:].rearrange("p c r t -> p (c r t)"),
            )
            return codes, scales

        def multiply(codes, scales):
            banks = []
            for m in range(M_TILES):
                rows = slice(m * P, (m + 1) * P)
                acc = acc_psum.tile([P, CHUNK], F32, name="acc")
                for c in range(PASSES):
                    nc.tensor.matmul_mx(
                        out=acc[:],
                        lhsT=g_codes[:, c, rows].bitcast(E5M2_X4),
                        lhsT_scale=g_scales[:, c, rows],
                        rhs=codes[:, c, :].bitcast(E4M3_X4),
                        rhs_scale=scales[:, c, :],
                        start=(c == 0),
                        stop=(c == PASSES - 1),
                    )
                banks.append(acc)
            return banks

        def store(n, m, copy, acc):
            result = stage.tile([P, CHUNK], F32)
            copy(out=result[:], in_=acc[:])
            nc.sync.dma_start(
                out=out[m * P : (m + 1) * P, n * CHUNK : (n + 1) * CHUNK], in_=result[:]
            )

        a_twice = {}
        b_flat = b_packed[:].rearrange("p r t -> p (r t)")
        b_first = {}
        for n in range(FIRST):
            a_twice[n] = spread_a(n)
            for v in range(2):
                bank = acc_psum.tile([P, HALF * PACK], BF16, name="acc")
                for w in range(2):
                    nc.tensor.matmul(
                        out=bank[:, w * CHUNK : (w + 1) * CHUNK],
                        lhsT=repeat[:, n, :],
                        rhs=b_flat[:, (2 * v + w) * CHUNK : (2 * v + w + 1) * CHUNK],
                        start=True,
                        stop=True,
                    )
                b_first[n, v] = bank
        regroup_on_gpsimd(nc, g_grouped[:, 1], g_rows[:, 1])
        regroup_on_vector(nc, g_grouped[:, 0], g_rows[:, 0])

        grouped = {}
        for n in range(N_CHUNKS + 1):
            if n + B_AHEAD < N_CHUNKS:
                load_b(n + B_AHEAD)
            if n < N_CHUNKS:
                grouped[n] = work.tile(
                    [P, PASSES, CHUNK, PACK], BF16, align_bytes=64, name="grouped"
                )
                split = CHUNK if all_in_sbuf(n) else CHUNK - G_COLS
                if n < FIRST:
                    for c in range(PASSES):
                        for v in range(2):
                            products_of(
                                nc.vector,
                                b_first[n, v][:],
                                c,
                                a_twice[n][c],
                                grouped[n],
                                v * HALF,
                                (v + 1) * HALF,
                            )
                else:
                    if split < CHUNK:
                        products(nc.gpsimd, n, 1, a_twice[n][1], grouped[n], split, CHUNK)
                    products(nc.vector, n, 0, a_twice[n][0], grouped[n], 0, CHUNK)
            if n + 2 < N_CHUNKS and n + 2 >= FIRST:
                a_twice[n + 2] = spread_a(n + 2)
            if FIRST <= n < N_CHUNKS - 1:
                products(nc.vector, n, 1, a_twice[n][1], grouped[n], 0, split)
            if n == 1:
                nc.vector.quantize_mx(
                    out=g_codes[:].rearrange("p c k -> p (c k)").bitcast(E5M2_X4),
                    scales=g_scales[:].rearrange("p c k -> p (c k)"),
                    in_=g_grouped[:].rearrange("p c k t -> p (c k t)"),
                )
            if n >= 1:
                codes, scales = quantise(grouped[n - 1])
                if n == N_CHUNKS - 1:
                    products(nc.vector, n, 1, a_twice[n][1], grouped[n], 0, split)
                banks = multiply(codes, scales)
                for m in range(M_TILES):
                    last = n == N_CHUNKS and m % 2 == 1
                    store(n - 1, m, nc.vector.tensor_copy if last else nc.scalar.copy, banks[m])
